import numpy as np
import ml_dtypes


def mxq(x, axis, fmt="e4m3"):
    dtype, down = {"e4m3": (ml_dtypes.float8_e4m3fn, 7), "e5m2": (ml_dtypes.float8_e5m2, 14)}[fmt]
    v = np.moveaxis(np.asarray(x, np.float32).astype(ml_dtypes.bfloat16).astype(np.float64), axis, -1)
    blocks = v.reshape(v.shape[:-1] + (-1, 32))
    amax = np.abs(blocks).max(-1, keepdims=True)
    byte = np.maximum(np.where(amax > 0, np.frexp(amax)[1] - 1 + 127, 0) - down, 1)
    scale = np.exp2(byte - 127.0)
    codes = (blocks / scale).astype(np.float32).astype(dtype).astype(np.float64)
    return np.moveaxis((codes * scale).reshape(v.shape), -1, axis)


WIDE = False


def mx_kscale(k):
    if not WIDE:
        return np.ones(k)
    levels = np.array([10, -10, 5, -5, 0])
    a = np.random.permutation(np.resize(levels, k // 512 * 4)).reshape(k // 512, 4)
    idx = np.arange(k)
    return np.exp2(a[idx // 512, idx % 128 // 32])


BF16 = ml_dtypes.bfloat16


def bf(x):
    return np.asarray(x, np.float32).astype(BF16)


def f64(x):
    return np.asarray(x).astype(np.float64)


E2M1 = np.array([0.0, 0.5, 1.0, 1.5, 2.0, 3.0, 4.0, 6.0, -0.0, -0.5, -1.0, -1.5, -2.0, -3.0, -4.0, -6.0])


def pack_weight(w, fmt):
    k, n = w.shape
    w = f64(bf(w)).reshape(k // 32, 32, n)
    amax = np.abs(w).max(1)
    if fmt == "e4m3":
        byte = np.frexp(amax)[1] - 1 + 127 - 7
    else:
        mant, ex = np.frexp(amax / 6.0)
        byte = np.where(mant > 0.5, ex, ex - 1) + 127
    byte = np.clip(np.where(amax > 0, byte, 1), 1, 254)
    scaled = (w * np.exp2(127.0 - byte)[:, None, :]).reshape(k, n).astype(np.float32)
    by_word = np.ascontiguousarray(scaled.reshape(k // 512, 128, 4, n).transpose(0, 1, 3, 2))
    if fmt == "e4m3":
        words = by_word.astype(ml_dtypes.float8_e4m3fn).view(np.uint8)
    else:
        c = by_word.astype(ml_dtypes.float4_e2m1fn).view(np.uint8) & 0xF
        words = c[..., 0::2] | (c[..., 1::2] << 4)
    return np.ascontiguousarray(words), np.ascontiguousarray(byte.astype(np.uint8).reshape(k // 512, 16, n))


def unpack_weight(words, scales, fmt):
    g, p, n, _ = words.shape
    if fmt == "e4m3":
        vals = np.ascontiguousarray(words).view(ml_dtypes.float8_e4m3fn).astype(np.float64)
    else:
        nib = np.empty((g, p, n, 4), np.uint8)
        nib[..., 0::2] = words & 0xF
        nib[..., 1::2] = words >> 4
        vals = E2M1[nib]
    vals = vals * np.repeat(np.exp2(scales.astype(np.float64) - 127.0), 8, axis=1)[..., None]
    return vals.transpose(0, 1, 3, 2).reshape(g * 512, n)


B, I, H = 128, 2048, 2048
EPS = 1e-5
FMT = "e4m3"


def sigmoid(v):
    return 1.0 / (1.0 + np.exp(-v))


def ln(v, g, b):
    m = v.mean(-1, keepdims=True)
    var = np.square(v - m).mean(-1, keepdims=True)
    return (v - m) / np.sqrt(var + EPS) * g + b


def setup_inputs():
    s, t = mx_kscale(I), mx_kscale(H)
    d = {"x": bf(np.random.standard_normal((B, I)) * s), "h": bf(np.random.standard_normal((B, H)) * t)}
    for g in ("i", "c"):
        words, scales = pack_weight((np.random.standard_normal((H, I)) / np.sqrt(I) / s[None, :]).T, FMT)
        d["W" + g + "_w_words"] = words
        d["W" + g + "_w_scales"] = scales
        d["W" + g + "_b"] = bf(np.random.standard_normal(H) * 0.5)
        words, scales = pack_weight((np.random.standard_normal((H, H)) / np.sqrt(H) / t[None, :]).T, FMT)
        d["U" + g + "_w_words"] = words
        d["U" + g + "_w_scales"] = scales
        d["ln" + g + "_g"] = bf(1.0 + 0.2 * np.random.standard_normal(H))
        d["ln" + g + "_b"] = bf(0.2 * np.random.standard_normal(H))
    return d


def reference(x, h, Wi_w_words, Wi_w_scales, Wi_b, Ui_w_words, Ui_w_scales, lni_g, lni_b, Wc_w_words, Wc_w_scales, Wc_b, Uc_w_words, Uc_w_scales, lnc_g, lnc_b):
    xq = mxq(f64(x), 1, "e4m3")
    hq = mxq(f64(h), 1, "e4m3")
    pre_i = (xq @ unpack_weight(Wi_w_words, Wi_w_scales, FMT)) + f64(Wi_b) + (hq @ unpack_weight(Ui_w_words, Ui_w_scales, FMT))
    pre_c = (xq @ unpack_weight(Wc_w_words, Wc_w_scales, FMT)) + f64(Wc_b) + (hq @ unpack_weight(Uc_w_words, Uc_w_scales, FMT))
    i = sigmoid(ln(pre_i, f64(lni_g), f64(lni_b)))
    c_tilde = np.tanh(ln(pre_c, f64(lnc_g), f64(lnc_b)))
    return i * c_tilde

@@ -1,0 +1,254 @@
+from contextlib import ExitStack
+
+import concourse.mybir as mybir
+from concourse.masks import make_identity
+
+F32 = mybir.dt.float32
+BF16 = mybir.dt.bfloat16
+I32 = mybir.dt.int32
+U32 = mybir.dt.uint32
+U8 = mybir.dt.uint8
+FP8X4 = mybir.dt.float8_e4m3fn_x4
+ALU = mybir.AluOpType
+ACT = mybir.ActivationFunctionType
+
+P = 128
+PACK = 4
+K_PASS = P * PACK
+FEATURES = 2048
+PASSES = FEATURES // K_PASS
+HIDDEN = 2048
+BLOCK = 512
+BLOCKS = HIDDEN // BLOCK
+QUADRANTS = 4
+EPS = 1e-5
+
+FLOPS = 4 * 2 * P * FEATURES * HIDDEN
+
+
+def block_cols(j):
+    return slice(j * BLOCK, (j + 1) * BLOCK)
+
+
+def tile_layernormlstmcell_pa_kernel(
+    tc,
+    x,
+    h,
+    Wi_w_words,
+    Wi_w_scales,
+    Wi_b,
+    Ui_w_words,
+    Ui_w_scales,
+    lni_g,
+    lni_b,
+    Wc_w_words,
+    Wc_w_scales,
+    Wc_b,
+    Uc_w_words,
+    Uc_w_scales,
+    lnc_g,
+    lnc_b,
+    out,
+):
+    nc = tc.nc
+    with ExitStack() as ctx:
+        ctx.enter_context(tc.manual_schedule())
+        keep = ctx.enter_context(tc.tile_pool(name="keep", bufs=1))
+        weights = ctx.enter_context(tc.tile_pool(name="weights", bufs=1))
+        psum = ctx.enter_context(tc.psum_pool(name="psum", bufs=8))
+
+        vec_rows = keep.tile([P, HIDDEN], BF16)
+        nc.vector.memset(vec_rows[:], 0.0)
+        w_planes = keep.tile([P, 4, HIDDEN], U8, align_bytes=64)
+        nc.vector.memset(w_planes[:].bitcast(I32), 0)
+
+        x_sb = keep.tile([P, FEATURES], BF16)
+        h_sb = keep.tile([P, FEATURES], BF16)
+        nc.sync.dma_start(out=x_sb[:], in_=x)
+        nc.sync.dma_start(out=h_sb[:], in_=h)
+
+        for r, vec in enumerate((Wi_b, lni_g, lni_b, Wc_b, lnc_g, lnc_b)):
+            nc.scalar.dma_start(out=vec_rows[r : r + 1, :], in_=vec.unsqueeze(0))
+
+        for w, scales in enumerate((Wi_w_scales, Ui_w_scales, Wc_w_scales, Uc_w_scales)):
+            for quad in range(QUADRANTS):
+                nc.sync.dma_start(
+                    out=w_planes[32 * quad : 32 * quad + 16, w, :].bitcast(I32),
+                    in_=scales[:, 4 * quad : 4 * quad + 4, :].bitcast(I32),
+                )
+
+        def load_words(words, g, first, width, name):
+            piece = weights.tile([P, width], U32, name=name, align_bytes=64)
+            nc.sync.dma_start(
+                out=piece[:].bitcast(I32),
+                in_=words[g, :, first : first + width, :].rearrange("p n t -> p (n t)").bitcast(I32),
+            )
+            return piece
+
+        wi = [load_words(Wi_w_words, g, 0, HIDDEN, "wi%d" % g) for g in range(PASSES)]
+        ui = [load_words(Ui_w_words, g, 0, HIDDEN, "ui%d" % g) for g in range(PASSES)]
+        wc = [load_words(Wc_w_words, g, 0, HIDDEN, "wc%d" % g) for g in range(PASSES)]
+        uc = [
+            [load_words(Uc_w_words, g, j * BLOCK, BLOCK, "uc%d_%d" % (j, g)) for g in range(PASSES)]
+            for j in range(BLOCKS)
+        ]
+
+        ident_f32 = keep.tile([P, P], F32)
+        make_identity(nc, ident_f32[:])
+        ident_bf16 = keep.tile([P, P], BF16)
+        make_identity(nc, ident_bf16[:])
+        minus_half = keep.tile([P, 1], F32)
+        nc.gpsimd.memset(minus_half[:], -0.5)
+
+        def transpose_words(src, name):
+            src_words = src[:].bitcast(F32)
+            grouped = keep.tile([P, PASSES, P, PACK], BF16, name=name, align_bytes=64)
+            grouped_words = grouped[:].bitcast(F32)
+            for first in range(0, PASSES, 2):
+                bank = psum.tile([P, 2, 2, P], F32, tag="bank", name="t_" + name)
+                for gg in range(2):
+                    start = (first + gg) * (K_PASS // 2)
+                    for u in range(2):
+                        nc.tensor.transpose(
+                            bank[:, gg, u, :],
+                            src_words[:, start + u : start + K_PASS // 2 : 2],
+                            ident_f32[:],
+                        )
+                nc.vector.tensor_copy(
+                    out=grouped_words[:, first : first + 2],
+                    in_=bank[:].rearrange("p g u b -> p g b u"),
+                )
+            return grouped
+
+        def quantise(grouped, name):
+            codes = keep.tile([P, PASSES * P], U32, name=name + "_codes", align_bytes=64)
+            plane = keep.tile([P, PASSES * P], U8, name=name + "_plane", align_bytes=64)
+            nc.vector.quantize_mx(
+                out=codes[:].bitcast(FP8X4),
+                scales=plane[:],
+                in_=grouped[:].rearrange("p g b t -> p (g b t)"),
+            )
+            return codes, plane
+
+        x_grouped = transpose_words(x_sb, "x_grouped")
+        h_grouped = transpose_words(h_sb, "h_grouped")
+        x_q = quantise(x_grouped, "x")
+        h_q = quantise(h_grouped, "h")
+
+        def spread(r, name):
+            wide = keep.tile([P, HIDDEN], BF16, name=name)
+            for first in range(0, BLOCKS, 2):
+                bank = psum.tile([P, 2 * BLOCK], BF16, tag="bank", name="s_" + name)
+                for jj in range(2):
+                    nc.tensor.matmul(
+                        out=bank[:, block_cols(jj)],
+                        lhsT=ident_bf16[:, r : r + 1].to_broadcast([P, P]),
+                        rhs=vec_rows[:, block_cols(first + jj)],
+                        start=True,
+                        stop=True,
+                    )
+                nc.scalar.copy(out=wide[:, first * BLOCK : (first + 2) * BLOCK], in_=bank[:])
+            return wide
+
+        bias_i, gain_i, shift_i = spread(0, "bias_i"), spread(1, "gain_i"), spread(2, "shift_i")
+        bias_c, gain_c, shift_c = spread(3, "bias_c"), spread(4, "gain_c"), spread(5, "shift_c")
+
+        def mx_pass(acc, act_q, g, piece, cols, w, j, start, stop):
+            codes, plane = act_q
+            batch = slice(g * P, (g + 1) * P)
+            nc.tensor.matmul_mx(
+                out=acc[:],
+                lhsT=codes[:, batch].bitcast(FP8X4),
+                lhsT_scale=plane[:, batch],
+                rhs=piece[:, cols].bitcast(FP8X4),
+                rhs_scale=w_planes[4 * g : P, w, block_cols(j)],
+                start=start,
+                stop=stop,
+            )
+
+        def add_bias(pre, acc, bias, j):
+            nc.vector.tensor_tensor(
+                out=pre[:, block_cols(j)], in0=acc[:], in1=bias[:, block_cols(j)], op=ALU.add
+            )
+
+        def block_stats(stats, pre, j):
+            nc.vector.bn_stats(out=stats[:, j, :], in_=pre[:, block_cols(j)])
+
+        def mean_and_rstd(stats, name):
+            mean_var = keep.tile([P, 2], F32, name=name + "_mean_var")
+            nc.vector.bn_aggr(out=mean_var[:], in_=stats[:].rearrange("p j s -> p (j s)"))
+            var_eps = keep.tile([P, 1], F32, name=name + "_var_eps")
+            rstd = keep.tile([P, 1], F32, name=name + "_rstd")
+            nc.gpsimd.tensor_scalar(
+                out=var_eps[:], in0=mean_var[:, 1:2], scalar1=EPS, scalar2=None, op0=ALU.add
+            )
+            nc.gpsimd.tensor_tensor(out=rstd[:], in0=var_eps[:], in1=minus_half[:], op=ALU.pow)
+            return mean_var[:, 0:1], rstd[:, 0:1]
+
+        def centre_times_gain(pre, mean, gain, j):
+            cols = block_cols(j)
+            nc.vector.scalar_tensor_tensor(
+                out=pre[:, cols], in0=pre[:, cols], scalar=mean, in1=gain[:, cols],
+                op0=ALU.subtract, op1=ALU.mult,
+            )
+
+        def scale_plus_shift(pre, rstd, shift, j):
+            cols = block_cols(j)
+            nc.vector.scalar_tensor_tensor(
+                out=pre[:, cols], in0=pre[:, cols], scalar=rstd, in1=shift[:, cols],
+                op0=ALU.mult, op1=ALU.add,
+            )
+
+        acc_i = [psum.tile([P, BLOCK], F32, tag="bank", name="acc_i%d" % j) for j in range(BLOCKS)]
+        for g in range(PASSES):
+            for j in range(BLOCKS):
+                mx_pass(acc_i[j], x_q, g, wi[g], block_cols(j), 0, j, start=(g == 0), stop=False)
+        for g in range(PASSES):
+            for j in range(BLOCKS):
+                mx_pass(
+                    acc_i[j], h_q, g, ui[g], block_cols(j), 1, j, start=False, stop=(g == PASSES - 1)
+                )
+
+        gate_i = keep.tile([P, HIDDEN], F32)
+        stats_i = keep.tile([P, BLOCKS, 6], F32)
+        for j in range(BLOCKS):
+            add_bias(gate_i, acc_i[j], bias_i, j)
+        for j in range(BLOCKS):
+            block_stats(stats_i, gate_i, j)
+        mean_i, rstd_i = mean_and_rstd(stats_i, "i")
+        for j in range(BLOCKS):
+            centre_times_gain(gate_i, mean_i, gain_i, j)
+        for j in range(BLOCKS):
+            scale_plus_shift(gate_i, rstd_i, shift_i, j)
+            nc.scalar.activation(
+                out=gate_i[:, block_cols(j)], in_=gate_i[:, block_cols(j)], func=ACT.Sigmoid
+            )
+
+        acc_c = [psum.tile([P, BLOCK], F32, tag="bank", name="acc_c%d" % j) for j in range(BLOCKS)]
+        for g in range(PASSES):
+            for j in range(BLOCKS):
+                mx_pass(acc_c[j], x_q, g, wc[g], block_cols(j), 2, j, start=(g == 0), stop=False)
+
+        cand = keep.tile([P, HIDDEN], F32)
+        stats_c = keep.tile([P, BLOCKS, 6], F32)
+        for j in range(BLOCKS):
+            for g in range(PASSES):
+                mx_pass(
+                    acc_c[j], h_q, g, uc[j][g], block_cols(0), 3, j, start=False, stop=(g == PASSES - 1)
+                )
+            add_bias(cand, acc_c[j], bias_c, j)
+            block_stats(stats_c, cand, j)
+        mean_c, rstd_c = mean_and_rstd(stats_c, "c")
+        for j in range(BLOCKS):
+            centre_times_gain(cand, mean_c, gain_c, j)
+        for j in range(BLOCKS):
+            scale_plus_shift(cand, rstd_c, shift_c, j)
+            nc.scalar.activation(
+                out=cand[:, block_cols(j)], in_=cand[:, block_cols(j)], func=ACT.Tanh
+            )
+        for j in range(BLOCKS):
+            cols = block_cols(j)
+            nc.vector.tensor_tensor(
+                out=cand[:, cols], in0=cand[:, cols], in1=gate_i[:, cols], op=ALU.mult
+            )
+            nc.sync.dma_start(out=out[:, cols], in_=cand[:, cols])

@@ -57,18 +57,24 @@ def tile_layernormlstmcell_pa_kernel(
         weights = ctx.enter_context(tc.tile_pool(name="weights", bufs=1))
         psum = ctx.enter_context(tc.psum_pool(name="psum", bufs=8))
 
-        vec_rows = keep.tile([P, HIDDEN], BF16)
-        nc.vector.memset(vec_rows[:], 0.0)
         w_planes = keep.tile([P, 4, HIDDEN], U8, align_bytes=64)
         nc.vector.memset(w_planes[:].bitcast(I32), 0)
+        vec_rows = keep.tile([P, HIDDEN], BF16)
+        nc.vector.memset(vec_rows[:], 0.0)
 
         x_sb = keep.tile([P, FEATURES], BF16)
         h_sb = keep.tile([P, FEATURES], BF16)
         nc.sync.dma_start(out=x_sb[:], in_=x)
         nc.sync.dma_start(out=h_sb[:], in_=h)
 
+        ident_f32 = keep.tile([P, P], F32)
+        make_identity(nc, ident_f32[:])
         for r, vec in enumerate((Wi_b, lni_g, lni_b, Wc_b, lnc_g, lnc_b)):
-            nc.scalar.dma_start(out=vec_rows[r : r + 1, :], in_=vec.unsqueeze(0))
+            nc.gpsimd.dma_start(out=vec_rows[r : r + 1, :], in_=vec.unsqueeze(0))
+        ident_bf16 = keep.tile([P, P], BF16)
+        make_identity(nc, ident_bf16[:])
+        minus_half = keep.tile([P, 1], F32)
+        nc.gpsimd.memset(minus_half[:], -0.5)
 
         for w, scales in enumerate((Wi_w_scales, Ui_w_scales, Wc_w_scales, Uc_w_scales)):
             for quad in range(QUADRANTS):
@@ -92,13 +98,6 @@ def tile_layernormlstmcell_pa_kernel(
             [load_words(Uc_w_words, g, j * BLOCK, BLOCK, "uc%d_%d" % (j, g)) for g in range(PASSES)]
             for j in range(BLOCKS)
         ]
-
-        ident_f32 = keep.tile([P, P], F32)
-        make_identity(nc, ident_f32[:])
-        ident_bf16 = keep.tile([P, P], BF16)
-        make_identity(nc, ident_bf16[:])
-        minus_half = keep.tile([P, 1], F32)
-        nc.gpsimd.memset(minus_half[:], -0.5)
 
         def transpose_words(src, name):
             src_words = src[:].bitcast(F32)

@@ -20,6 +20,7 @@ PASSES = FEATURES // K_PASS
 HIDDEN = 2048
 BLOCK = 512
 BLOCKS = HIDDEN // BLOCK
+ROWS = 8
 QUADRANTS = 4
 EPS = 1e-5
 
@@ -55,12 +56,15 @@ def tile_layernormlstmcell_pa_kernel(
         ctx.enter_context(tc.manual_schedule())
         keep = ctx.enter_context(tc.tile_pool(name="keep", bufs=1))
         weights = ctx.enter_context(tc.tile_pool(name="weights", bufs=1))
-        psum = ctx.enter_context(tc.psum_pool(name="psum", bufs=8))
+        psum_i = ctx.enter_context(tc.psum_pool(name="psum_i", bufs=4))
+        psum = ctx.enter_context(tc.psum_pool(name="psum", bufs=4))
 
         w_planes = keep.tile([P, 4, HIDDEN], U8, align_bytes=64)
         nc.vector.memset(w_planes[:].bitcast(I32), 0)
         vec_rows = keep.tile([P, HIDDEN], BF16)
-        nc.vector.memset(vec_rows[:], 0.0)
+        nc.vector.memset(vec_rows[:].bitcast(I32), 0)
+        coef = keep.tile([P, P], BF16)
+        nc.vector.memset(coef[:].bitcast(I32), 0)
 
         x_sb = keep.tile([P, FEATURES], BF16)
         h_sb = keep.tile([P, FEATURES], BF16)
@@ -69,12 +73,12 @@ def tile_layernormlstmcell_pa_kernel(
 
         ident_f32 = keep.tile([P, P], F32)
         make_identity(nc, ident_f32[:])
-        for r, vec in enumerate((Wi_b, lni_g, lni_b, Wc_b, lnc_g, lnc_b)):
-            nc.gpsimd.dma_start(out=vec_rows[r : r + 1, :], in_=vec.unsqueeze(0))
         ident_bf16 = keep.tile([P, P], BF16)
         make_identity(nc, ident_bf16[:])
         minus_half = keep.tile([P, 1], F32)
         nc.gpsimd.memset(minus_half[:], -0.5)
+        half = keep.tile([P, 1], F32)
+        nc.gpsimd.memset(half[:], 0.5)
 
         for w, scales in enumerate((Wi_w_scales, Ui_w_scales, Wc_w_scales, Uc_w_scales)):
             for quad in range(QUADRANTS):
@@ -91,7 +95,12 @@ def tile_layernormlstmcell_pa_kernel(
             )
             return piece
 
-        wi = [load_words(Wi_w_words, g, 0, HIDDEN, "wi%d" % g) for g in range(PASSES)]
+        vectors = (Wi_b, lni_g, lni_b, Wc_b, lnc_g, lnc_b, lnc_g, lnc_b)
+        wi = []
+        for g in range(PASSES):
+            wi.append(load_words(Wi_w_words, g, 0, HIDDEN, "wi%d" % g))
+            for r in (2 * g, 2 * g + 1):
+                nc.sync.dma_start(out=vec_rows[r : r + 1, :], in_=vectors[r].unsqueeze(0))
         ui = [load_words(Ui_w_words, g, 0, HIDDEN, "ui%d" % g) for g in range(PASSES)]
         wc = [load_words(Wc_w_words, g, 0, HIDDEN, "wc%d" % g) for g in range(PASSES)]
         uc = [
@@ -134,23 +143,39 @@ def tile_layernormlstmcell_pa_kernel(
         x_q = quantise(x_grouped, "x")
         h_q = quantise(h_grouped, "h")
 
+        word_chunks = HIDDEN // 2 // P
+        vec_cols = keep.tile([P, word_chunks * ROWS], F32)
+
+        def turn_vectors():
+            vec_words = vec_rows[:].bitcast(F32)
+            for first in range(0, word_chunks, 4):
+                bank = psum.tile([P, 4, P], F32, tag="bank", name="vec_bank")
+                for c in range(4):
+                    nc.tensor.transpose(
+                        bank[:, c, :], vec_words[:, (first + c) * P : (first + c + 1) * P], ident_f32[:]
+                    )
+                nc.vector.tensor_copy(
+                    out=vec_cols[:, first * ROWS : (first + 4) * ROWS].rearrange(
+                        "p (c r) -> p c r", r=ROWS
+                    ),
+                    in_=bank[:, :, 0:ROWS],
+                )
+
         def spread(r, name):
             wide = keep.tile([P, HIDDEN], BF16, name=name)
-            for first in range(0, BLOCKS, 2):
-                bank = psum.tile([P, 2 * BLOCK], BF16, tag="bank", name="s_" + name)
-                for jj in range(2):
-                    nc.tensor.matmul(
-                        out=bank[:, block_cols(jj)],
-                        lhsT=ident_bf16[:, r : r + 1].to_broadcast([P, P]),
-                        rhs=vec_rows[:, block_cols(first + jj)],
-                        start=True,
-                        stop=True,
+            wide_words = wide[:].bitcast(F32)
+            for first in range(0, word_chunks, 4):
+                bank = psum.tile([P, 4, P], F32, tag="bank", name="s_" + name)
+                for c in range(4):
+                    col = (first + c) * ROWS + r
+                    nc.tensor.transpose(
+                        bank[:, c, :], vec_cols[:, col : col + 1].to_broadcast([P, P]), ident_f32[:]
                     )
-                nc.scalar.copy(out=wide[:, first * BLOCK : (first + 2) * BLOCK], in_=bank[:])
+                nc.scalar.copy(
+                    out=wide_words[:, first * P : (first + 4) * P],
+                    in_=bank[:].rearrange("p c w -> p (c w)"),
+                )
             return wide
-
-        bias_i, gain_i, shift_i = spread(0, "bias_i"), spread(1, "gain_i"), spread(2, "shift_i")
-        bias_c, gain_c, shift_c = spread(3, "bias_c"), spread(4, "gain_c"), spread(5, "shift_c")
 
         def mx_pass(acc, act_q, g, piece, cols, w, j, start, stop):
             codes, plane = act_q
@@ -198,10 +223,13 @@ def tile_layernormlstmcell_pa_kernel(
                 op0=ALU.mult, op1=ALU.add,
             )
 
-        acc_i = [psum.tile([P, BLOCK], F32, tag="bank", name="acc_i%d" % j) for j in range(BLOCKS)]
+        acc_i = [psum_i.tile([P, BLOCK], F32, tag="bank", name="acc_i%d" % j) for j in range(BLOCKS)]
         for g in range(PASSES):
             for j in range(BLOCKS):
                 mx_pass(acc_i[j], x_q, g, wi[g], block_cols(j), 0, j, start=(g == 0), stop=False)
+        turn_vectors()
+        bias_i, gain_i, shift_i = spread(0, "bias_i"), spread(1, "gain_i"), spread(2, "shift_i")
+        bias_c, gain_c = spread(3, "bias_c"), spread(4, "gain_c")
         for g in range(PASSES):
             for j in range(BLOCKS):
                 mx_pass(
@@ -229,22 +257,63 @@ def tile_layernormlstmcell_pa_kernel(
                 mx_pass(acc_c[j], x_q, g, wc[g], block_cols(j), 2, j, start=(g == 0), stop=False)
 
         cand = keep.tile([P, HIDDEN], F32)
+        scaled = keep.tile([P, HIDDEN], F32)
         stats_c = keep.tile([P, BLOCKS, 6], F32)
+        mean_var = keep.tile([P, 2], F32)
+        var_eps = keep.tile([P, 1], F32)
+        std = keep.tile([P, 1], F32)
+        rstd_c = keep.tile([P, 1], F32)
+        coef_rows = keep.tile([P, P], BF16)
+        arg = [psum_i.tile([P, BLOCK], F32, tag="bank", name="arg%d" % j) for j in range(BLOCKS)]
+
+        def scale_block(j):
+            cols = block_cols(j)
+            nc.vector.tensor_tensor(
+                out=scaled[:, cols], in0=cand[:, cols], in1=gain_c[:, cols], op=ALU.mult
+            )
+
+        def open_arg(j):
+            nc.tensor.matmul(
+                out=arg[j][:], lhsT=ident_f32[:], rhs=scaled[:, block_cols(j)], start=True, stop=False
+            )
+
         for j in range(BLOCKS):
             for g in range(PASSES):
                 mx_pass(
                     acc_c[j], h_q, g, uc[j][g], block_cols(0), 3, j, start=False, stop=(g == PASSES - 1)
                 )
+            if j > 0:
+                open_arg(j - 1)
             add_bias(cand, acc_c[j], bias_c, j)
             block_stats(stats_c, cand, j)
-        mean_c, rstd_c = mean_and_rstd(stats_c, "c")
+            if j < BLOCKS - 1:
+                scale_block(j)
+
+        nc.vector.bn_aggr(out=mean_var[:], in_=stats_c[:].rearrange("p j s -> p (j s)"))
+        mean = mean_var[:, 0:1]
+        nc.gpsimd.tensor_scalar(
+            out=var_eps[:], in0=mean_var[:, 1:2], scalar1=EPS, scalar2=None, op0=ALU.add
+        )
+        nc.gpsimd.tensor_tensor(out=std[:], in0=var_eps[:], in1=half[:], op=ALU.pow)
+        nc.gpsimd.tensor_tensor(out=rstd_c[:], in0=var_eps[:], in1=minus_half[:], op=ALU.pow)
+        scale_block(BLOCKS - 1)
+        open_arg(BLOCKS - 1)
+        nc.vector.tensor_scalar(out=coef[:, 4:5], in0=mean, scalar1=-1.0, scalar2=None, op0=ALU.mult)
+        nc.vector.scalar_tensor_tensor(
+            out=coef[:, 6:7], in0=mean, scalar=-1.0, in1=coef[:, 4:5], op0=ALU.mult, op1=ALU.subtract
+        )
+        nc.vector.tensor_copy(out=coef[:, 5:6], in_=std[:])
+        nc.vector.tensor_tensor(out=coef[:, 7:8], in0=std[:], in1=coef[:, 5:6], op=ALU.subtract)
+        turned = psum.tile([P, P], BF16, tag="bank", name="turned")
+        nc.tensor.transpose(turned[:], coef[:], ident_bf16[:])
+        nc.vector.tensor_copy(out=coef_rows[:], in_=turned[:])
+
         for j in range(BLOCKS):
-            centre_times_gain(cand, mean_c, gain_c, j)
-        for j in range(BLOCKS):
-            scale_plus_shift(cand, rstd_c, shift_c, j)
-            nc.scalar.activation(
-                out=cand[:, block_cols(j)], in_=cand[:, block_cols(j)], func=ACT.Tanh
+            cols = block_cols(j)
+            nc.tensor.matmul(
+                out=arg[j][:], lhsT=coef_rows[:], rhs=vec_rows[:, cols], start=False, stop=True
             )
+            nc.scalar.activation(out=cand[:, cols], in_=arg[j][:], func=ACT.Tanh, scale=rstd_c[:])
         for j in range(BLOCKS):
             cols = block_cols(j)
             nc.vector.tensor_tensor(

@@ -162,15 +162,15 @@ def tile_layernormlstmcell_pa_kernel(
                 )
 
         def spread(r, name):
+            columns = keep.tile([P, word_chunks, P], F32, name="columns_" + name)
+            picked = vec_cols[:].rearrange("p (c r) -> p c r", r=ROWS)[:, :, r : r + 1]
+            nc.vector.tensor_copy(out=columns[:], in_=picked.to_broadcast([P, word_chunks, P]))
             wide = keep.tile([P, HIDDEN], BF16, name=name)
             wide_words = wide[:].bitcast(F32)
             for first in range(0, word_chunks, 4):
                 bank = psum.tile([P, 4, P], F32, tag="bank", name="s_" + name)
                 for c in range(4):
-                    col = (first + c) * ROWS + r
-                    nc.tensor.transpose(
-                        bank[:, c, :], vec_cols[:, col : col + 1].to_broadcast([P, P]), ident_f32[:]
-                    )
+                    nc.tensor.transpose(bank[:, c, :], columns[:, first + c, :], ident_f32[:])
                 nc.scalar.copy(
                     out=wide_words[:, first * P : (first + 4) * P],
                     in_=bank[:].rearrange("p c w -> p (c w)"),
@@ -266,6 +266,8 @@ def tile_layernormlstmcell_pa_kernel(
         coef_rows = keep.tile([P, P], BF16)
         arg = [psum_i.tile([P, BLOCK], F32, tag="bank", name="arg%d" % j) for j in range(BLOCKS)]
 
+        last = BLOCKS - 1
+
         def scale_block(j):
             cols = block_cols(j)
             nc.vector.tensor_tensor(
@@ -296,8 +298,7 @@ def tile_layernormlstmcell_pa_kernel(
         )
         nc.gpsimd.tensor_tensor(out=std[:], in0=var_eps[:], in1=half[:], op=ALU.pow)
         nc.gpsimd.tensor_tensor(out=rstd_c[:], in0=var_eps[:], in1=minus_half[:], op=ALU.pow)
-        scale_block(BLOCKS - 1)
-        open_arg(BLOCKS - 1)
+        scale_block(last)
         nc.vector.tensor_scalar(out=coef[:, 4:5], in0=mean, scalar1=-1.0, scalar2=None, op0=ALU.mult)
         nc.vector.scalar_tensor_tensor(
             out=coef[:, 6:7], in0=mean, scalar=-1.0, in1=coef[:, 4:5], op0=ALU.mult, op1=ALU.subtract
@@ -308,12 +309,27 @@ def tile_layernormlstmcell_pa_kernel(
         nc.tensor.transpose(turned[:], coef[:], ident_bf16[:])
         nc.vector.tensor_copy(out=coef_rows[:], in_=turned[:])
 
-        for j in range(BLOCKS):
-            cols = block_cols(j)
+        def close_arg(j):
             nc.tensor.matmul(
-                out=arg[j][:], lhsT=coef_rows[:], rhs=vec_rows[:, cols], start=False, stop=True
+                out=arg[j][:], lhsT=coef_rows[:], rhs=vec_rows[:, block_cols(j)],
+                start=(j == last), stop=True,
             )
-            nc.scalar.activation(out=cand[:, cols], in_=arg[j][:], func=ACT.Tanh, scale=rstd_c[:])
+
+        def tanh(j, source):
+            nc.scalar.activation(
+                out=cand[:, block_cols(j)], in_=source, func=ACT.Tanh, scale=rstd_c[:]
+            )
+
+        close_arg(0)
+        close_arg(last)
+        for j in range(1, last):
+            close_arg(j)
+        for j in range(last):
+            tanh(j, arg[j][:])
+        nc.vector.tensor_tensor(
+            out=scaled[:, block_cols(last)], in0=arg[last][:], in1=scaled[:, block_cols(last)], op=ALU.add
+        )
+        tanh(last, scaled[:, block_cols(last)])
         for j in range(BLOCKS):
             cols = block_cols(j)
             nc.vector.tensor_tensor(

@@ -20,8 +20,8 @@ PASSES = FEATURES // K_PASS
 HIDDEN = 2048
 BLOCK = 512
 BLOCKS = HIDDEN // BLOCK
-ROWS = 8
-QUADRANTS = 4
+QUADRANT = 32
+QUADRANTS = P // QUADRANT
 EPS = 1e-5
 
 FLOPS = 4 * 2 * P * FEATURES * HIDDEN
@@ -61,7 +61,7 @@ def tile_layernormlstmcell_pa_kernel(
 
         w_planes = keep.tile([P, 4, HIDDEN], U8, align_bytes=64)
         nc.vector.memset(w_planes[:].bitcast(I32), 0)
-        vec_rows = keep.tile([P, HIDDEN], BF16)
+        vec_rows = keep.tile([P, HIDDEN], BF16, align_bytes=64)
         nc.vector.memset(vec_rows[:].bitcast(I32), 0)
         coef = keep.tile([P, P], BF16)
         nc.vector.memset(coef[:].bitcast(I32), 0)
@@ -95,12 +95,14 @@ def tile_layernormlstmcell_pa_kernel(
             )
             return piece
 
-        vectors = (Wi_b, lni_g, lni_b, Wc_b, lnc_g, lnc_b, lnc_g, lnc_b)
+        vectors = (Wi_b, lni_g, lni_b, Wc_b, lnc_g, lnc_b)
         wi = []
         for g in range(PASSES):
             wi.append(load_words(Wi_w_words, g, 0, HIDDEN, "wi%d" % g))
-            for r in (2 * g, 2 * g + 1):
-                nc.sync.dma_start(out=vec_rows[r : r + 1, :], in_=vectors[r].unsqueeze(0))
+            for r in range(2 * g, min(2 * g + 2, len(vectors))):
+                nc.sync.dma_start(
+                    out=vec_rows[r:P:QUADRANT, :], in_=vectors[r].partition_broadcast(QUADRANTS)
+                )
         ui = [load_words(Ui_w_words, g, 0, HIDDEN, "ui%d" % g) for g in range(PASSES)]
         wc = [load_words(Wc_w_words, g, 0, HIDDEN, "wc%d" % g) for g in range(PASSES)]
         uc = [
@@ -143,38 +145,18 @@ def tile_layernormlstmcell_pa_kernel(
         x_q = quantise(x_grouped, "x")
         h_q = quantise(h_grouped, "h")
 
-        word_chunks = HIDDEN // 2 // P
-        vec_cols = keep.tile([P, word_chunks * ROWS], F32)
-
-        def turn_vectors():
-            vec_words = vec_rows[:].bitcast(F32)
-            for first in range(0, word_chunks, 4):
-                bank = psum.tile([P, 4, P], F32, tag="bank", name="vec_bank")
-                for c in range(4):
-                    nc.tensor.transpose(
-                        bank[:, c, :], vec_words[:, (first + c) * P : (first + c + 1) * P], ident_f32[:]
-                    )
-                nc.vector.tensor_copy(
-                    out=vec_cols[:, first * ROWS : (first + 4) * ROWS].rearrange(
-                        "p (c r) -> p c r", r=ROWS
-                    ),
-                    in_=bank[:, :, 0:ROWS],
-                )
+        words = HIDDEN // 2
+        turned_rows = keep.tile([P, words], F32, align_bytes=64)
 
         def spread(r, name):
-            columns = keep.tile([P, word_chunks, P], F32, name="columns_" + name)
-            picked = vec_cols[:].rearrange("p (c r) -> p c r", r=ROWS)[:, :, r : r + 1]
-            nc.vector.tensor_copy(out=columns[:], in_=picked.to_broadcast([P, word_chunks, P]))
-            wide = keep.tile([P, HIDDEN], BF16, name=name)
-            wide_words = wide[:].bitcast(F32)
-            for first in range(0, word_chunks, 4):
-                bank = psum.tile([P, 4, P], F32, tag="bank", name="s_" + name)
-                for c in range(4):
-                    nc.tensor.transpose(bank[:, c, :], columns[:, first + c, :], ident_f32[:])
-                nc.scalar.copy(
-                    out=wide_words[:, first * P : (first + 4) * P],
-                    in_=bank[:].rearrange("p c w -> p (c w)"),
-                )
+            repeated = keep.tile([P, words], F32, name="repeated_" + name, align_bytes=64)
+            picked = turned_rows[:].rearrange("p (b r) -> p b r", r=QUADRANT)[:, :, r : r + 1]
+            nc.scalar.copy(
+                out=repeated[:].rearrange("p (b i) -> p b i", i=QUADRANT),
+                in_=picked.to_broadcast([P, words // QUADRANT, QUADRANT]),
+            )
+            wide = keep.tile([P, HIDDEN], BF16, name=name, align_bytes=64)
+            nc.vector.transpose(out=wide[:].bitcast(F32), in_=repeated[:])
             return wide
 
         def mx_pass(acc, act_q, g, piece, cols, w, j, start, stop):
@@ -227,7 +209,7 @@ def tile_layernormlstmcell_pa_kernel(
         for g in range(PASSES):
             for j in range(BLOCKS):
                 mx_pass(acc_i[j], x_q, g, wi[g], block_cols(j), 0, j, start=(g == 0), stop=False)
-        turn_vectors()
+        nc.vector.transpose(out=turned_rows[:], in_=vec_rows[:].bitcast(F32))
         bias_i, gain_i, shift_i = spread(0, "bias_i"), spread(1, "gain_i"), spread(2, "shift_i")
         bias_c, gain_c = spread(3, "bias_c"), spread(4, "gain_c")
         for g in range(PASSES):
@@ -299,12 +281,14 @@ def tile_layernormlstmcell_pa_kernel(
         nc.gpsimd.tensor_tensor(out=std[:], in0=var_eps[:], in1=half[:], op=ALU.pow)
         nc.gpsimd.tensor_tensor(out=rstd_c[:], in0=var_eps[:], in1=minus_half[:], op=ALU.pow)
         scale_block(last)
-        nc.vector.tensor_scalar(out=coef[:, 4:5], in0=mean, scalar1=-1.0, scalar2=None, op0=ALU.mult)
+        gain_hi, gain_lo = coef[:, 4:5], coef[:, QUADRANT + 4 : QUADRANT + 5]
+        shift_hi, shift_lo = coef[:, 5:6], coef[:, QUADRANT + 5 : QUADRANT + 6]
+        nc.vector.tensor_scalar(out=gain_hi, in0=mean, scalar1=-1.0, scalar2=None, op0=ALU.mult)
         nc.vector.scalar_tensor_tensor(
-            out=coef[:, 6:7], in0=mean, scalar=-1.0, in1=coef[:, 4:5], op0=ALU.mult, op1=ALU.subtract
+            out=gain_lo, in0=mean, scalar=-1.0, in1=gain_hi, op0=ALU.mult, op1=ALU.subtract
         )
-        nc.vector.tensor_copy(out=coef[:, 5:6], in_=std[:])
-        nc.vector.tensor_tensor(out=coef[:, 7:8], in0=std[:], in1=coef[:, 5:6], op=ALU.subtract)
+        nc.vector.tensor_copy(out=shift_hi, in_=std[:])
+        nc.vector.tensor_tensor(out=shift_lo, in0=std[:], in1=shift_hi, op=ALU.subtract)
         turned = psum.tile([P, P], BF16, tag="bank", name="turned")
         nc.tensor.transpose(turned[:], coef[:], ident_bf16[:])
         nc.vector.tensor_copy(out=coef_rows[:], in_=turned[:])

@@ -24,6 +24,10 @@ QUADRANT = 32
 QUADRANTS = P // QUADRANT
 EPS = 1e-5
 
+CAND_BLOCKS = ((0, 512), (512, 512), (1024, 512), (1536, 256), (1792, 256))
+TENSOR_BLOCKS = 3
+U_RANGES = ((0, 1024), (1024, 512), (1536, 256), (1792, 256))
+
 FLOPS = 4 * 2 * P * FEATURES * HIDDEN
 
 
@@ -55,13 +59,14 @@ def tile_layernormlstmcell_pa_kernel(
     with ExitStack() as ctx:
         ctx.enter_context(tc.manual_schedule())
         keep = ctx.enter_context(tc.tile_pool(name="keep", bufs=1))
+        stage = ctx.enter_context(tc.tile_pool(name="stage", bufs=2))
         weights = ctx.enter_context(tc.tile_pool(name="weights", bufs=1))
         psum_i = ctx.enter_context(tc.psum_pool(name="psum_i", bufs=4))
         psum = ctx.enter_context(tc.psum_pool(name="psum", bufs=4))
 
         w_planes = keep.tile([P, 4, HIDDEN], U8, align_bytes=64)
         nc.vector.memset(w_planes[:].bitcast(I32), 0)
-        vec_rows = keep.tile([P, HIDDEN], BF16, align_bytes=64)
+        vec_rows = keep.tile([P, HIDDEN], BF16)
         nc.vector.memset(vec_rows[:].bitcast(I32), 0)
         coef = keep.tile([P, P], BF16)
         nc.vector.memset(coef[:].bitcast(I32), 0)
@@ -73,12 +78,12 @@ def tile_layernormlstmcell_pa_kernel(
 
         ident_f32 = keep.tile([P, P], F32)
         make_identity(nc, ident_f32[:])
+        for r, vec in enumerate((Wi_b, lni_g, lni_b, Wc_b, lnc_g, lnc_b)):
+            nc.gpsimd.dma_start(out=vec_rows[r : r + 1, :], in_=vec.unsqueeze(0))
         ident_bf16 = keep.tile([P, P], BF16)
         make_identity(nc, ident_bf16[:])
         minus_half = keep.tile([P, 1], F32)
         nc.gpsimd.memset(minus_half[:], -0.5)
-        half = keep.tile([P, 1], F32)
-        nc.gpsimd.memset(half[:], 0.5)
 
         for w, scales in enumerate((Wi_w_scales, Ui_w_scales, Wc_w_scales, Uc_w_scales)):
             for quad in range(QUADRANTS):
@@ -95,20 +100,14 @@ def tile_layernormlstmcell_pa_kernel(
             )
             return piece
 
-        vectors = (Wi_b, lni_g, lni_b, Wc_b, lnc_g, lnc_b)
-        wi = []
-        for g in range(PASSES):
-            wi.append(load_words(Wi_w_words, g, 0, HIDDEN, "wi%d" % g))
-            for r in range(2 * g, min(2 * g + 2, len(vectors))):
-                nc.sync.dma_start(
-                    out=vec_rows[r:P:QUADRANT, :], in_=vectors[r].partition_broadcast(QUADRANTS)
-                )
+        wi = [load_words(Wi_w_words, g, 0, HIDDEN, "wi%d" % g) for g in range(PASSES)]
         ui = [load_words(Ui_w_words, g, 0, HIDDEN, "ui%d" % g) for g in range(PASSES)]
-        wc = [load_words(Wc_w_words, g, 0, HIDDEN, "wc%d" % g) for g in range(PASSES)]
-        uc = [
-            [load_words(Uc_w_words, g, j * BLOCK, BLOCK, "uc%d_%d" % (j, g)) for g in range(PASSES)]
-            for j in range(BLOCKS)
-        ]
+        wc, uc = [], []
+        for first, width in ((0, 1024), (1024, 1024)):
+            wc.append((first, [load_words(Wc_w_words, g, first, width, "wc%d_%d" % (first, g)) for g in range(PASSES)]))
+            for start, cut in U_RANGES:
+                if first <= start < first + width:
+                    uc.append((start, [load_words(Uc_w_words, g, start, cut, "uc%d_%d" % (start, g)) for g in range(PASSES)]))
 
         def transpose_words(src, name):
             src_words = src[:].bitcast(F32)
@@ -145,11 +144,33 @@ def tile_layernormlstmcell_pa_kernel(
         x_q = quantise(x_grouped, "x")
         h_q = quantise(h_grouped, "h")
 
+        quadrant_picks = keep.tile([P, P], BF16)
+        nc.vector.tensor_copy(
+            out=quadrant_picks[:].rearrange("p (q c) -> p q c", c=QUADRANT),
+            in_=ident_bf16[:, 0:QUADRANT].unsqueeze(1).to_broadcast([P, QUADRANTS, QUADRANT]),
+        )
+        vec_quads = keep.tile([P, HIDDEN], BF16, align_bytes=64)
+
+        def repeat_quadrant():
+            for first in range(0, BLOCKS, 2):
+                bank = psum.tile([P, 2 * BLOCK], BF16, tag="bank", name="quads")
+                for jj in range(2):
+                    nc.tensor.matmul(
+                        out=bank[:, block_cols(jj)],
+                        lhsT=quadrant_picks[:],
+                        rhs=vec_rows[:, block_cols(first + jj)],
+                        start=True,
+                        stop=True,
+                    )
+                nc.scalar.copy(
+                    out=vec_quads[:, first * BLOCK : (first + 2) * BLOCK], in_=bank[:]
+                )
+
         words = HIDDEN // 2
         turned_rows = keep.tile([P, words], F32, align_bytes=64)
 
         def spread(r, name):
-            repeated = keep.tile([P, words], F32, name="repeated_" + name, align_bytes=64)
+            repeated = stage.tile([P, words], F32, tag="repeated", name="repeated", align_bytes=64)
             picked = turned_rows[:].rearrange("p (b r) -> p b r", r=QUADRANT)[:, :, r : r + 1]
             nc.scalar.copy(
                 out=repeated[:].rearrange("p (b i) -> p b i", i=QUADRANT),
@@ -159,26 +180,29 @@ def tile_layernormlstmcell_pa_kernel(
             nc.vector.transpose(out=wide[:].bitcast(F32), in_=repeated[:])
             return wide
 
-        def mx_pass(acc, act_q, g, piece, cols, w, j, start, stop):
+        repeat_quadrant()
+        nc.vector.transpose(out=turned_rows[:], in_=vec_quads[:].bitcast(F32))
+        bias_i, gain_i, shift_i = spread(0, "bias_i"), spread(1, "gain_i"), spread(2, "shift_i")
+        bias_c, gain_c, shift_c = spread(3, "bias_c"), spread(4, "gain_c"), spread(5, "shift_c")
+
+        def mx_pass(acc, act_q, g, piece, first, w, cols, start, stop):
             codes, plane = act_q
             batch = slice(g * P, (g + 1) * P)
             nc.tensor.matmul_mx(
                 out=acc[:],
                 lhsT=codes[:, batch].bitcast(FP8X4),
                 lhsT_scale=plane[:, batch],
-                rhs=piece[:, cols].bitcast(FP8X4),
-                rhs_scale=w_planes[4 * g : P, w, block_cols(j)],
+                rhs=piece[:, cols.start - first : cols.stop - first].bitcast(FP8X4),
+                rhs_scale=w_planes[4 * g : P, w, cols],
                 start=start,
                 stop=stop,
             )
 
-        def add_bias(pre, acc, bias, j):
-            nc.vector.tensor_tensor(
-                out=pre[:, block_cols(j)], in0=acc[:], in1=bias[:, block_cols(j)], op=ALU.add
-            )
+        def add_bias(pre, acc, bias, cols):
+            nc.vector.tensor_tensor(out=pre[:, cols], in0=acc[:], in1=bias[:, cols], op=ALU.add)
 
-        def block_stats(stats, pre, j):
-            nc.vector.bn_stats(out=stats[:, j, :], in_=pre[:, block_cols(j)])
+        def block_stats(stats, pre, j, cols):
+            nc.vector.bn_stats(out=stats[:, j, :], in_=pre[:, cols])
 
         def mean_and_rstd(stats, name):
             mean_var = keep.tile([P, 2], F32, name=name + "_mean_var")
@@ -191,15 +215,13 @@ def tile_layernormlstmcell_pa_kernel(
             nc.gpsimd.tensor_tensor(out=rstd[:], in0=var_eps[:], in1=minus_half[:], op=ALU.pow)
             return mean_var[:, 0:1], rstd[:, 0:1]
 
-        def centre_times_gain(pre, mean, gain, j):
-            cols = block_cols(j)
+        def centre_times_gain(pre, mean, gain, cols):
             nc.vector.scalar_tensor_tensor(
                 out=pre[:, cols], in0=pre[:, cols], scalar=mean, in1=gain[:, cols],
                 op0=ALU.subtract, op1=ALU.mult,
             )
 
-        def scale_plus_shift(pre, rstd, shift, j):
-            cols = block_cols(j)
+        def scale_plus_shift(pre, rstd, shift, cols):
             nc.vector.scalar_tensor_tensor(
                 out=pre[:, cols], in0=pre[:, cols], scalar=rstd, in1=shift[:, cols],
                 op0=ALU.mult, op1=ALU.add,
@@ -208,114 +230,123 @@ def tile_layernormlstmcell_pa_kernel(
         acc_i = [psum_i.tile([P, BLOCK], F32, tag="bank", name="acc_i%d" % j) for j in range(BLOCKS)]
         for g in range(PASSES):
             for j in range(BLOCKS):
-                mx_pass(acc_i[j], x_q, g, wi[g], block_cols(j), 0, j, start=(g == 0), stop=False)
-        nc.vector.transpose(out=turned_rows[:], in_=vec_rows[:].bitcast(F32))
-        bias_i, gain_i, shift_i = spread(0, "bias_i"), spread(1, "gain_i"), spread(2, "shift_i")
-        bias_c, gain_c = spread(3, "bias_c"), spread(4, "gain_c")
+                mx_pass(acc_i[j], x_q, g, wi[g], 0, 0, block_cols(j), start=(g == 0), stop=False)
         for g in range(PASSES):
             for j in range(BLOCKS):
                 mx_pass(
-                    acc_i[j], h_q, g, ui[g], block_cols(j), 1, j, start=False, stop=(g == PASSES - 1)
+                    acc_i[j], h_q, g, ui[g], 0, 1, block_cols(j), start=False, stop=(g == PASSES - 1)
                 )
 
         gate_i = keep.tile([P, HIDDEN], F32)
         stats_i = keep.tile([P, BLOCKS, 6], F32)
         for j in range(BLOCKS):
-            add_bias(gate_i, acc_i[j], bias_i, j)
+            add_bias(gate_i, acc_i[j], bias_i, block_cols(j))
         for j in range(BLOCKS):
-            block_stats(stats_i, gate_i, j)
+            block_stats(stats_i, gate_i, j, block_cols(j))
         mean_i, rstd_i = mean_and_rstd(stats_i, "i")
         for j in range(BLOCKS):
-            centre_times_gain(gate_i, mean_i, gain_i, j)
+            centre_times_gain(gate_i, mean_i, gain_i, block_cols(j))
         for j in range(BLOCKS):
-            scale_plus_shift(gate_i, rstd_i, shift_i, j)
+            scale_plus_shift(gate_i, rstd_i, shift_i, block_cols(j))
             nc.scalar.activation(
                 out=gate_i[:, block_cols(j)], in_=gate_i[:, block_cols(j)], func=ACT.Sigmoid
             )
 
-        acc_c = [psum.tile([P, BLOCK], F32, tag="bank", name="acc_c%d" % j) for j in range(BLOCKS)]
-        for g in range(PASSES):
-            for j in range(BLOCKS):
-                mx_pass(acc_c[j], x_q, g, wc[g], block_cols(j), 2, j, start=(g == 0), stop=False)
-
         cand = keep.tile([P, HIDDEN], F32)
-        scaled = keep.tile([P, HIDDEN], F32)
-        stats_c = keep.tile([P, BLOCKS, 6], F32)
+        scaled = keep.tile([P, TENSOR_BLOCKS * BLOCK], F32)
+        stats_c = keep.tile([P, len(CAND_BLOCKS), 6], F32)
         mean_var = keep.tile([P, 2], F32)
         var_eps = keep.tile([P, 1], F32)
-        std = keep.tile([P, 1], F32)
-        rstd_c = keep.tile([P, 1], F32)
+        rstd = keep.tile([P, 1], F32)
         coef_rows = keep.tile([P, P], BF16)
-        arg = [psum_i.tile([P, BLOCK], F32, tag="bank", name="arg%d" % j) for j in range(BLOCKS)]
+        cand_cols = [slice(first, first + width) for first, width in CAND_BLOCKS]
+        on_tensor, on_vector = cand_cols[:TENSOR_BLOCKS], cand_cols[TENSOR_BLOCKS:]
 
-        last = BLOCKS - 1
+        acc_c = {}
 
-        def scale_block(j):
-            cols = block_cols(j)
-            nc.vector.tensor_tensor(
+        def x_passes(half):
+            first, pieces = wc[half]
+            for g in range(PASSES):
+                for b, cols in enumerate(cand_cols):
+                    if first <= cols.start < first + HIDDEN // 2:
+                        if g == 0:
+                            pool = psum_i if b == len(cand_cols) - 1 else psum
+                            acc = pool.tile([P, cols.stop - cols.start], F32, tag="bank", name="acc_c%d" % b)
+                            acc_c[b] = acc
+                        mx_pass(acc_c[b], x_q, g, pieces[g], first, 2, cols, start=(g == 0), stop=False)
+
+        def h_passes(load):
+            first, pieces = uc[load]
+            for g in range(PASSES):
+                for b, cols in enumerate(cand_cols):
+                    if first <= cols.start < first + U_RANGES[load][1]:
+                        mx_pass(
+                            acc_c[b], h_q, g, pieces[g], first, 3, cols,
+                            start=False, stop=(g == PASSES - 1),
+                        )
+
+        def pre_and_stats(b):
+            add_bias(cand, acc_c[b], bias_c, cand_cols[b])
+            block_stats(stats_c, cand, b, cand_cols[b])
+
+        arg = []
+
+        def open_arg(b):
+            cols = cand_cols[b]
+            nc.gpsimd.tensor_tensor(
                 out=scaled[:, cols], in0=cand[:, cols], in1=gain_c[:, cols], op=ALU.mult
             )
-
-        def open_arg(j):
+            bank = psum_i.tile([P, BLOCK], F32, tag="bank", name="arg%d" % b)
             nc.tensor.matmul(
-                out=arg[j][:], lhsT=ident_f32[:], rhs=scaled[:, block_cols(j)], start=True, stop=False
+                out=bank[:], lhsT=ident_f32[:], rhs=scaled[:, cols], start=True, stop=False
             )
+            arg.append(bank)
 
-        for j in range(BLOCKS):
-            for g in range(PASSES):
-                mx_pass(
-                    acc_c[j], h_q, g, uc[j][g], block_cols(0), 3, j, start=False, stop=(g == PASSES - 1)
-                )
-            if j > 0:
-                open_arg(j - 1)
-            add_bias(cand, acc_c[j], bias_c, j)
-            block_stats(stats_c, cand, j)
-            if j < BLOCKS - 1:
-                scale_block(j)
+        x_passes(0)
+        h_passes(0)
+        pre_and_stats(0)
+        pre_and_stats(1)
+        x_passes(1)
+        open_arg(0)
+        open_arg(1)
+        h_passes(1)
+        pre_and_stats(2)
+        h_passes(2)
+        pre_and_stats(3)
+        h_passes(3)
+        pre_and_stats(4)
+        open_arg(2)
 
         nc.vector.bn_aggr(out=mean_var[:], in_=stats_c[:].rearrange("p j s -> p (j s)"))
         mean = mean_var[:, 0:1]
-        nc.gpsimd.tensor_scalar(
+        nc.vector.tensor_scalar(
             out=var_eps[:], in0=mean_var[:, 1:2], scalar1=EPS, scalar2=None, op0=ALU.add
         )
-        nc.gpsimd.tensor_tensor(out=std[:], in0=var_eps[:], in1=half[:], op=ALU.pow)
-        nc.gpsimd.tensor_tensor(out=rstd_c[:], in0=var_eps[:], in1=minus_half[:], op=ALU.pow)
-        scale_block(last)
+        nc.gpsimd.tensor_tensor(out=rstd[:], in0=var_eps[:], in1=minus_half[:], op=ALU.pow)
+        for cols in on_vector:
+            centre_times_gain(cand, mean, gain_c, cols)
         gain_hi, gain_lo = coef[:, 4:5], coef[:, QUADRANT + 4 : QUADRANT + 5]
         shift_hi, shift_lo = coef[:, 5:6], coef[:, QUADRANT + 5 : QUADRANT + 6]
         nc.vector.tensor_scalar(out=gain_hi, in0=mean, scalar1=-1.0, scalar2=None, op0=ALU.mult)
         nc.vector.scalar_tensor_tensor(
             out=gain_lo, in0=mean, scalar=-1.0, in1=gain_hi, op0=ALU.mult, op1=ALU.subtract
         )
-        nc.vector.tensor_copy(out=shift_hi, in_=std[:])
-        nc.vector.tensor_tensor(out=shift_lo, in0=std[:], in1=shift_hi, op=ALU.subtract)
+        nc.vector.tensor_tensor(out=shift_hi, in0=var_eps[:], in1=rstd[:], op=ALU.mult)
+        nc.vector.scalar_tensor_tensor(
+            out=shift_lo, in0=var_eps[:], scalar=rstd[:], in1=shift_hi, op0=ALU.mult, op1=ALU.subtract
+        )
         turned = psum.tile([P, P], BF16, tag="bank", name="turned")
         nc.tensor.transpose(turned[:], coef[:], ident_bf16[:])
-        nc.vector.tensor_copy(out=coef_rows[:], in_=turned[:])
-
-        def close_arg(j):
+        nc.scalar.copy(out=coef_rows[:], in_=turned[:])
+        for cols in on_vector:
+            scale_plus_shift(cand, rstd[:], shift_c, cols)
+            nc.scalar.activation(out=cand[:, cols], in_=cand[:, cols], func=ACT.Tanh)
+        for bank, cols in zip(arg, on_tensor):
             nc.tensor.matmul(
-                out=arg[j][:], lhsT=coef_rows[:], rhs=vec_rows[:, block_cols(j)],
-                start=(j == last), stop=True,
+                out=bank[:], lhsT=coef_rows[:], rhs=vec_quads[:, cols], start=False, stop=True
             )
-
-        def tanh(j, source):
-            nc.scalar.activation(
-                out=cand[:, block_cols(j)], in_=source, func=ACT.Tanh, scale=rstd_c[:]
-            )
-
-        close_arg(0)
-        close_arg(last)
-        for j in range(1, last):
-            close_arg(j)
-        for j in range(last):
-            tanh(j, arg[j][:])
-        nc.vector.tensor_tensor(
-            out=scaled[:, block_cols(last)], in0=arg[last][:], in1=scaled[:, block_cols(last)], op=ALU.add
-        )
-        tanh(last, scaled[:, block_cols(last)])
-        for j in range(BLOCKS):
-            cols = block_cols(j)
+            nc.scalar.activation(out=cand[:, cols], in_=bank[:], func=ACT.Tanh, scale=rstd[:])
+        for cols in on_vector + on_tensor:
             nc.vector.tensor_tensor(
                 out=cand[:, cols], in0=cand[:, cols], in1=gate_i[:, cols], op=ALU.mult
             )

@@ -64,10 +64,10 @@ def tile_layernormlstmcell_pa_kernel(
         psum_i = ctx.enter_context(tc.psum_pool(name="psum_i", bufs=4))
         psum = ctx.enter_context(tc.psum_pool(name="psum", bufs=4))
 
-        w_planes = keep.tile([P, 4, HIDDEN], U8, align_bytes=64)
-        nc.vector.memset(w_planes[:].bitcast(I32), 0)
         vec_rows = keep.tile([P, HIDDEN], BF16)
         nc.vector.memset(vec_rows[:].bitcast(I32), 0)
+        w_planes = keep.tile([P, 4, HIDDEN], U8, align_bytes=64)
+        nc.vector.memset(w_planes[:].bitcast(I32), 0)
         coef = keep.tile([P, P], BF16)
         nc.vector.memset(coef[:].bitcast(I32), 0)
 
@@ -78,10 +78,10 @@ def tile_layernormlstmcell_pa_kernel(
 
         ident_f32 = keep.tile([P, P], F32)
         make_identity(nc, ident_f32[:])
-        for r, vec in enumerate((Wi_b, lni_g, lni_b, Wc_b, lnc_g, lnc_b)):
-            nc.gpsimd.dma_start(out=vec_rows[r : r + 1, :], in_=vec.unsqueeze(0))
         ident_bf16 = keep.tile([P, P], BF16)
         make_identity(nc, ident_bf16[:])
+        for r, vec in enumerate((Wi_b, lni_g, lni_b, Wc_b, lnc_g, lnc_b)):
+            nc.gpsimd.dma_start(out=vec_rows[r : r + 1, :], in_=vec.unsqueeze(0))
         minus_half = keep.tile([P, 1], F32)
         nc.gpsimd.memset(minus_half[:], -0.5)
 
@@ -246,11 +246,13 @@ def tile_layernormlstmcell_pa_kernel(
         mean_i, rstd_i = mean_and_rstd(stats_i, "i")
         for j in range(BLOCKS):
             centre_times_gain(gate_i, mean_i, gain_i, block_cols(j))
-        for j in range(BLOCKS):
-            scale_plus_shift(gate_i, rstd_i, shift_i, block_cols(j))
-            nc.scalar.activation(
-                out=gate_i[:, block_cols(j)], in_=gate_i[:, block_cols(j)], func=ACT.Sigmoid
-            )
+
+        def finish_gate():
+            for j in range(BLOCKS):
+                scale_plus_shift(gate_i, rstd_i, shift_i, block_cols(j))
+                nc.scalar.activation(
+                    out=gate_i[:, block_cols(j)], in_=gate_i[:, block_cols(j)], func=ACT.Sigmoid
+                )
 
         cand = keep.tile([P, HIDDEN], F32)
         scaled = keep.tile([P, TENSOR_BLOCKS * BLOCK], F32)
@@ -264,9 +266,9 @@ def tile_layernormlstmcell_pa_kernel(
 
         acc_c = {}
 
-        def x_passes(half):
+        def x_passes(half, passes):
             first, pieces = wc[half]
-            for g in range(PASSES):
+            for g in passes:
                 for b, cols in enumerate(cand_cols):
                     if first <= cols.start < first + HIDDEN // 2:
                         if g == 0:
@@ -291,26 +293,34 @@ def tile_layernormlstmcell_pa_kernel(
 
         arg = []
 
-        def open_arg(b):
+        def scale_block(engine, b):
             cols = cand_cols[b]
-            nc.gpsimd.tensor_tensor(
+            engine.tensor_tensor(
                 out=scaled[:, cols], in0=cand[:, cols], in1=gain_c[:, cols], op=ALU.mult
             )
+
+        def open_arg(b):
+            cols = cand_cols[b]
             bank = psum_i.tile([P, BLOCK], F32, tag="bank", name="arg%d" % b)
             nc.tensor.matmul(
                 out=bank[:], lhsT=ident_f32[:], rhs=scaled[:, cols], start=True, stop=False
             )
             arg.append(bank)
 
-        x_passes(0)
+        x_passes(0, range(PASSES))
         h_passes(0)
-        pre_and_stats(0)
-        pre_and_stats(1)
-        x_passes(1)
+        for b in range(2):
+            pre_and_stats(b)
+            scale_block(nc.vector, b)
+        finish_gate()
+        x_passes(1, range(2))
         open_arg(0)
+        x_passes(1, range(2, 3))
         open_arg(1)
+        x_passes(1, range(3, PASSES))
         h_passes(1)
         pre_and_stats(2)
+        scale_block(nc.gpsimd, 2)
         h_passes(2)
         pre_and_stats(3)
         h_passes(3)
@@ -345,8 +355,16 @@ def tile_layernormlstmcell_pa_kernel(
             nc.tensor.matmul(
                 out=bank[:], lhsT=coef_rows[:], rhs=vec_quads[:, cols], start=False, stop=True
             )
-            nc.scalar.activation(out=cand[:, cols], in_=bank[:], func=ACT.Tanh, scale=rstd[:])
-        for cols in on_vector + on_tensor:
+        cut = BLOCK // 2
+        parts = [(arg[0], 0, BLOCK), (arg[1], 0, BLOCK), (arg[2], 0, cut), (arg[2], cut, BLOCK)]
+        finished = list(on_vector)
+        for b, (bank, start, stop) in zip((0, 1, 2, 2), parts):
+            cols = slice(b * BLOCK + start, b * BLOCK + stop)
+            nc.scalar.activation(
+                out=cand[:, cols], in_=bank[:, start:stop], func=ACT.Tanh, scale=rstd[:]
+            )
+            finished.append(cols)
+        for cols in finished:
             nc.vector.tensor_tensor(
                 out=cand[:, cols], in0=cand[:, cols], in1=gate_i[:, cols], op=ALU.mult
             )

@@ -73,6 +73,8 @@ def tile_layernormlstmcell_pa_kernel(
 
         x_sb = keep.tile([P, FEATURES], BF16)
         h_sb = keep.tile([P, FEATURES], BF16)
+        for r, vec in enumerate((Wi_b, lni_g, lni_b, Wc_b, lnc_g, lnc_b)):
+            nc.scalar.dma_start(out=vec_rows[r : r + 1, :], in_=vec.unsqueeze(0))
         nc.sync.dma_start(out=x_sb[:], in_=x)
         nc.sync.dma_start(out=h_sb[:], in_=h)
 
@@ -80,8 +82,6 @@ def tile_layernormlstmcell_pa_kernel(
         make_identity(nc, ident_f32[:])
         ident_bf16 = keep.tile([P, P], BF16)
         make_identity(nc, ident_bf16[:])
-        for r, vec in enumerate((Wi_b, lni_g, lni_b, Wc_b, lnc_g, lnc_b)):
-            nc.gpsimd.dma_start(out=vec_rows[r : r + 1, :], in_=vec.unsqueeze(0))
         minus_half = keep.tile([P, 1], F32)
         nc.gpsimd.memset(minus_half[:], -0.5)
 
@@ -212,7 +212,7 @@ def tile_layernormlstmcell_pa_kernel(
             nc.gpsimd.tensor_scalar(
                 out=var_eps[:], in0=mean_var[:, 1:2], scalar1=EPS, scalar2=None, op0=ALU.add
             )
-            nc.gpsimd.tensor_tensor(out=rstd[:], in0=var_eps[:], in1=minus_half[:], op=ALU.pow)
+            nc.gpsimd.tensor_tensor(out=rstd[:], in0=var_eps, in1=minus_half[:], op=ALU.pow)
             return mean_var[:, 0:1], rstd[:, 0:1]
 
         def centre_times_gain(pre, mean, gain, cols):
@@ -256,9 +256,13 @@ def tile_layernormlstmcell_pa_kernel(
 
         cand = keep.tile([P, HIDDEN], F32)
         scaled = keep.tile([P, TENSOR_BLOCKS * BLOCK], F32)
-        stats_c = keep.tile([P, len(CAND_BLOCKS), 6], F32)
+        stats_c = keep.tile([P, 6 * len(CAND_BLOCKS) + 3], F32)
+        eps_record = stats_c[:, 6 * len(CAND_BLOCKS) :]
+        nc.vector.memset(eps_record, 0.0)
+        nc.vector.tensor_scalar(
+            out=eps_record[:, 2:3], in0=eps_record[:, 2:3], scalar1=HIDDEN * EPS, scalar2=None, op0=ALU.add
+        )
         mean_var = keep.tile([P, 2], F32)
-        var_eps = keep.tile([P, 1], F32)
         rstd = keep.tile([P, 1], F32)
         coef_rows = keep.tile([P, P], BF16)
         cand_cols = [slice(first, first + width) for first, width in CAND_BLOCKS]
@@ -287,9 +291,11 @@ def tile_layernormlstmcell_pa_kernel(
                             start=False, stop=(g == PASSES - 1),
                         )
 
-        def pre_and_stats(b):
+        def add_block_bias(b):
             add_bias(cand, acc_c[b], bias_c, cand_cols[b])
-            block_stats(stats_c, cand, b, cand_cols[b])
+
+        def take_stats(b):
+            nc.vector.bn_stats(out=stats_c[:, 6 * b : 6 * b + 6], in_=cand[:, cand_cols[b]])
 
         arg = []
 
@@ -309,9 +315,12 @@ def tile_layernormlstmcell_pa_kernel(
 
         x_passes(0, range(PASSES))
         h_passes(0)
+        add_block_bias(0)
+        add_block_bias(1)
         for b in range(2):
-            pre_and_stats(b)
             scale_block(nc.vector, b)
+        for b in range(2):
+            take_stats(b)
         finish_gate()
         x_passes(1, range(2))
         open_arg(0)
@@ -319,38 +328,40 @@ def tile_layernormlstmcell_pa_kernel(
         open_arg(1)
         x_passes(1, range(3, PASSES))
         h_passes(1)
-        pre_and_stats(2)
+        add_block_bias(2)
         scale_block(nc.gpsimd, 2)
         h_passes(2)
-        pre_and_stats(3)
+        add_block_bias(3)
+        take_stats(2)
         h_passes(3)
-        pre_and_stats(4)
+        add_block_bias(4)
+        take_stats(3)
+        take_stats(4)
         open_arg(2)
 
-        nc.vector.bn_aggr(out=mean_var[:], in_=stats_c[:].rearrange("p j s -> p (j s)"))
-        mean = mean_var[:, 0:1]
-        nc.vector.tensor_scalar(
-            out=var_eps[:], in0=mean_var[:, 1:2], scalar1=EPS, scalar2=None, op0=ALU.add
-        )
-        nc.gpsimd.tensor_tensor(out=rstd[:], in0=var_eps[:], in1=minus_half[:], op=ALU.pow)
-        for cols in on_vector:
-            centre_times_gain(cand, mean, gain_c, cols)
+        nc.vector.bn_aggr(out=mean_var[:], in_=stats_c[:])
+        mean, var_eps = mean_var[:, 0:1], mean_var[:, 1:2]
+        nc.gpsimd.tensor_tensor(out=rstd[:], in0=var_eps, in1=minus_half[:], op=ALU.pow)
         gain_hi, gain_lo = coef[:, 4:5], coef[:, QUADRANT + 4 : QUADRANT + 5]
         shift_hi, shift_lo = coef[:, 5:6], coef[:, QUADRANT + 5 : QUADRANT + 6]
         nc.vector.tensor_scalar(out=gain_hi, in0=mean, scalar1=-1.0, scalar2=None, op0=ALU.mult)
+        centre_times_gain(cand, mean, gain_c, on_vector[0])
         nc.vector.scalar_tensor_tensor(
             out=gain_lo, in0=mean, scalar=-1.0, in1=gain_hi, op0=ALU.mult, op1=ALU.subtract
         )
-        nc.vector.tensor_tensor(out=shift_hi, in0=var_eps[:], in1=rstd[:], op=ALU.mult)
+        centre_times_gain(cand, mean, gain_c, on_vector[1])
+        nc.vector.tensor_tensor(out=shift_hi, in0=var_eps, in1=rstd[:], op=ALU.mult)
+        scale_plus_shift(cand, rstd[:], shift_c, on_vector[0])
         nc.vector.scalar_tensor_tensor(
-            out=shift_lo, in0=var_eps[:], scalar=rstd[:], in1=shift_hi, op0=ALU.mult, op1=ALU.subtract
+            out=shift_lo, in0=var_eps, scalar=rstd[:], in1=shift_hi, op0=ALU.mult, op1=ALU.subtract
         )
+        scale_plus_shift(cand, rstd[:], shift_c, on_vector[1])
         turned = psum.tile([P, P], BF16, tag="bank", name="turned")
         nc.tensor.transpose(turned[:], coef[:], ident_bf16[:])
-        nc.scalar.copy(out=coef_rows[:], in_=turned[:])
-        for cols in on_vector:
-            scale_plus_shift(cand, rstd[:], shift_c, cols)
+        for i, cols in enumerate(on_vector):
             nc.scalar.activation(out=cand[:, cols], in_=cand[:, cols], func=ACT.Tanh)
+            if i == 0:
+                nc.scalar.copy(out=coef_rows[:], in_=turned[:])
         for bank, cols in zip(arg, on_tensor):
             nc.tensor.matmul(
                 out=bank[:], lhsT=coef_rows[:], rhs=vec_quads[:, cols], start=False, stop=True

@@ -64,17 +64,15 @@ def tile_layernormlstmcell_pa_kernel(
         psum_i = ctx.enter_context(tc.psum_pool(name="psum_i", bufs=4))
         psum = ctx.enter_context(tc.psum_pool(name="psum", bufs=4))
 
-        vec_rows = keep.tile([P, HIDDEN], BF16)
-        nc.vector.memset(vec_rows[:].bitcast(I32), 0)
         w_planes = keep.tile([P, 4, HIDDEN], U8, align_bytes=64)
         nc.vector.memset(w_planes[:].bitcast(I32), 0)
+        vec_rows = keep.tile([P, HIDDEN], BF16)
+        nc.vector.memset(vec_rows[:].bitcast(I32), 0)
         coef = keep.tile([P, P], BF16)
         nc.vector.memset(coef[:].bitcast(I32), 0)
 
         x_sb = keep.tile([P, FEATURES], BF16)
         h_sb = keep.tile([P, FEATURES], BF16)
-        for r, vec in enumerate((Wi_b, lni_g, lni_b, Wc_b, lnc_g, lnc_b)):
-            nc.scalar.dma_start(out=vec_rows[r : r + 1, :], in_=vec.unsqueeze(0))
         nc.sync.dma_start(out=x_sb[:], in_=x)
         nc.sync.dma_start(out=h_sb[:], in_=h)
 
@@ -82,11 +80,13 @@ def tile_layernormlstmcell_pa_kernel(
         make_identity(nc, ident_f32[:])
         ident_bf16 = keep.tile([P, P], BF16)
         make_identity(nc, ident_bf16[:])
+        for r, vec in enumerate((Wi_b, lni_g, lni_b, Wc_b, lnc_g, lnc_b)):
+            nc.gpsimd.dma_start(out=vec_rows[r : r + 1, :], in_=vec.unsqueeze(0))
         minus_half = keep.tile([P, 1], F32)
         nc.gpsimd.memset(minus_half[:], -0.5)
 
-        for w, scales in enumerate((Wi_w_scales, Ui_w_scales, Wc_w_scales, Uc_w_scales)):
-            for quad in range(QUADRANTS):
+        for quad in (0, 2, 3, 1):
+            for w, scales in enumerate((Wi_w_scales, Ui_w_scales, Wc_w_scales, Uc_w_scales)):
                 nc.sync.dma_start(
                     out=w_planes[32 * quad : 32 * quad + 16, w, :].bitcast(I32),
                     in_=scales[:, 4 * quad : 4 * quad + 4, :].bitcast(I32),

@@ -92,22 +92,28 @@ def tile_layernormlstmcell_pa_kernel(
                     in_=scales[:, 4 * quad : 4 * quad + 4, :].bitcast(I32),
                 )
 
-        def load_words(words, g, first, width, name):
-            piece = weights.tile([P, width], U32, name=name, align_bytes=64)
-            nc.sync.dma_start(
-                out=piece[:].bitcast(I32),
-                in_=words[g, :, first : first + width, :].rearrange("p n t -> p (n t)").bitcast(I32),
-            )
-            return piece
+        def load_words(words, first, width, cuts, name):
+            passes = []
+            for count in cuts:
+                g = len(passes)
+                piece = weights.tile([P, count, width], U32, name="%s_%d" % (name, g), align_bytes=64)
+                nc.sync.dma_start(
+                    out=piece[:].bitcast(I32),
+                    in_=words[g : g + count, :, first : first + width, :]
+                    .rearrange("g p n t -> p g (n t)")
+                    .bitcast(I32),
+                )
+                passes.extend([piece[:, i, :] for i in range(count)])
+            return passes
 
-        wi = [load_words(Wi_w_words, g, 0, HIDDEN, "wi%d" % g) for g in range(PASSES)]
-        ui = [load_words(Ui_w_words, g, 0, HIDDEN, "ui%d" % g) for g in range(PASSES)]
+        wi = load_words(Wi_w_words, 0, HIDDEN, (2, 2), "wi")
+        ui = load_words(Ui_w_words, 0, HIDDEN, (2, 2), "ui")
         wc, uc = [], []
         for first, width in ((0, 1024), (1024, 1024)):
-            wc.append((first, [load_words(Wc_w_words, g, first, width, "wc%d_%d" % (first, g)) for g in range(PASSES)]))
+            wc.append((first, load_words(Wc_w_words, first, width, (2, 2), "wc%d" % first)))
             for start, cut in U_RANGES:
                 if first <= start < first + width:
-                    uc.append((start, [load_words(Uc_w_words, g, start, cut, "uc%d_%d" % (start, g)) for g in range(PASSES)]))
+                    uc.append((start, load_words(Uc_w_words, start, cut, (2, 2), "uc%d" % start)))
 
         def transpose_words(src, name):
             src_words = src[:].bitcast(F32)
@@ -324,9 +330,8 @@ def tile_layernormlstmcell_pa_kernel(
         finish_gate()
         x_passes(1, range(2))
         open_arg(0)
-        x_passes(1, range(2, 3))
         open_arg(1)
-        x_passes(1, range(3, PASSES))
+        x_passes(1, range(2, PASSES))
         h_passes(1)
         add_block_bias(2)
         scale_block(nc.gpsimd, 2)

from contextlib import ExitStack

import concourse.mybir as mybir
from concourse.masks import make_identity

F32 = mybir.dt.float32
BF16 = mybir.dt.bfloat16
I32 = mybir.dt.int32
U32 = mybir.dt.uint32
U8 = mybir.dt.uint8
FP8X4 = mybir.dt.float8_e4m3fn_x4
ALU = mybir.AluOpType
ACT = mybir.ActivationFunctionType

P = 128
PACK = 4
K_PASS = P * PACK
FEATURES = 2048
PASSES = FEATURES // K_PASS
HIDDEN = 2048
BLOCK = 512
BLOCKS = HIDDEN // BLOCK
QUADRANT = 32
QUADRANTS = P // QUADRANT
EPS = 1e-5

CAND_BLOCKS = ((0, 512), (512, 512), (1024, 512), (1536, 256), (1792, 256))
TENSOR_BLOCKS = 3
U_RANGES = ((0, 1024), (1024, 512), (1536, 256), (1792, 256))

FLOPS = 4 * 2 * P * FEATURES * HIDDEN


def block_cols(j):
    return slice(j * BLOCK, (j + 1) * BLOCK)


def tile_layernormlstmcell_pa_kernel(
    tc,
    x,
    h,
    Wi_w_words,
    Wi_w_scales,
    Wi_b,
    Ui_w_words,
    Ui_w_scales,
    lni_g,
    lni_b,
    Wc_w_words,
    Wc_w_scales,
    Wc_b,
    Uc_w_words,
    Uc_w_scales,
    lnc_g,
    lnc_b,
    out,
):
    nc = tc.nc
    with ExitStack() as ctx:
        ctx.enter_context(tc.manual_schedule())
        keep = ctx.enter_context(tc.tile_pool(name="keep", bufs=1))
        stage = ctx.enter_context(tc.tile_pool(name="stage", bufs=2))
        weights = ctx.enter_context(tc.tile_pool(name="weights", bufs=1))
        psum_i = ctx.enter_context(tc.psum_pool(name="psum_i", bufs=4))
        psum = ctx.enter_context(tc.psum_pool(name="psum", bufs=4))

        w_planes = keep.tile([P, 4, HIDDEN], U8, align_bytes=64)
        nc.vector.memset(w_planes[:].bitcast(I32), 0)
        vec_rows = keep.tile([P, HIDDEN], BF16)
        nc.vector.memset(vec_rows[:].bitcast(I32), 0)
        coef = keep.tile([P, P], BF16)
        nc.vector.memset(coef[:].bitcast(I32), 0)

        x_sb = keep.tile([P, FEATURES], BF16)
        h_sb = keep.tile([P, FEATURES], BF16)
        nc.sync.dma_start(out=x_sb[:], in_=x)
        nc.sync.dma_start(out=h_sb[:], in_=h)

        ident_f32 = keep.tile([P, P], F32)
        make_identity(nc, ident_f32[:])
        ident_bf16 = keep.tile([P, P], BF16)
        make_identity(nc, ident_bf16[:])
        for r, vec in enumerate((Wi_b, lni_g, lni_b, Wc_b, lnc_g, lnc_b)):
            nc.gpsimd.dma_start(out=vec_rows[r : r + 1, :], in_=vec.unsqueeze(0))
        minus_half = keep.tile([P, 1], F32)
        nc.gpsimd.memset(minus_half[:], -0.5)

        for quad in (0, 2, 3, 1):
            for w, scales in enumerate((Wi_w_scales, Ui_w_scales, Wc_w_scales, Uc_w_scales)):
                nc.sync.dma_start(
                    out=w_planes[32 * quad : 32 * quad + 16, w, :].bitcast(I32),
                    in_=scales[:, 4 * quad : 4 * quad + 4, :].bitcast(I32),
                )

        def load_words(words, first, width, cuts, name):
            passes = []
            for count in cuts:
                g = len(passes)
                piece = weights.tile([P, count, width], U32, name="%s_%d" % (name, g), align_bytes=64)
                nc.sync.dma_start(
                    out=piece[:].bitcast(I32),
                    in_=words[g : g + count, :, first : first + width, :]
                    .rearrange("g p n t -> p g (n t)")
                    .bitcast(I32),
                )
                passes.extend([piece[:, i, :] for i in range(count)])
            return passes

        wi = load_words(Wi_w_words, 0, HIDDEN, (2, 2), "wi")
        ui = load_words(Ui_w_words, 0, HIDDEN, (2, 2), "ui")
        wc, uc = [], []
        for first, width in ((0, 1024), (1024, 1024)):
            wc.append((first, load_words(Wc_w_words, first, width, (2, 2), "wc%d" % first)))
            for start, cut in U_RANGES:
                if first <= start < first + width:
                    uc.append((start, load_words(Uc_w_words, start, cut, (2, 2), "uc%d" % start)))

        def transpose_words(src, name):
            src_words = src[:].bitcast(F32)
            grouped = keep.tile([P, PASSES, P, PACK], BF16, name=name, align_bytes=64)
            grouped_words = grouped[:].bitcast(F32)
            for first in range(0, PASSES, 2):
                bank = psum.tile([P, 2, 2, P], F32, tag="bank", name="t_" + name)
                for gg in range(2):
                    start = (first + gg) * (K_PASS // 2)
                    for u in range(2):
                        nc.tensor.transpose(
                            bank[:, gg, u, :],
                            src_words[:, start + u : start + K_PASS // 2 : 2],
                            ident_f32[:],
                        )
                nc.vector.tensor_copy(
                    out=grouped_words[:, first : first + 2],
                    in_=bank[:].rearrange("p g u b -> p g b u"),
                )
            return grouped

        def quantise(grouped, name):
            codes = keep.tile([P, PASSES * P], U32, name=name + "_codes", align_bytes=64)
            plane = keep.tile([P, PASSES * P], U8, name=name + "_plane", align_bytes=64)
            nc.vector.quantize_mx(
                out=codes[:].bitcast(FP8X4),
                scales=plane[:],
                in_=grouped[:].rearrange("p g b t -> p (g b t)"),
            )
            return codes, plane

        x_grouped = transpose_words(x_sb, "x_grouped")
        h_grouped = transpose_words(h_sb, "h_grouped")
        x_q = quantise(x_grouped, "x")
        h_q = quantise(h_grouped, "h")

        quadrant_picks = keep.tile([P, P], BF16)
        nc.vector.tensor_copy(
            out=quadrant_picks[:].rearrange("p (q c) -> p q c", c=QUADRANT),
            in_=ident_bf16[:, 0:QUADRANT].unsqueeze(1).to_broadcast([P, QUADRANTS, QUADRANT]),
        )
        vec_quads = keep.tile([P, HIDDEN], BF16, align_bytes=64)

        def repeat_quadrant():
            for first in range(0, BLOCKS, 2):
                bank = psum.tile([P, 2 * BLOCK], BF16, tag="bank", name="quads")
                for jj in range(2):
                    nc.tensor.matmul(
                        out=bank[:, block_cols(jj)],
                        lhsT=quadrant_picks[:],
                        rhs=vec_rows[:, block_cols(first + jj)],
                        start=True,
                        stop=True,
                    )
                nc.scalar.copy(
                    out=vec_quads[:, first * BLOCK : (first + 2) * BLOCK], in_=bank[:]
                )

        words = HIDDEN // 2
        turned_rows = keep.tile([P, words], F32, align_bytes=64)

        def spread(r, name):
            repeated = stage.tile([P, words], F32, tag="repeated", name="repeated", align_bytes=64)
            picked = turned_rows[:].rearrange("p (b r) -> p b r", r=QUADRANT)[:, :, r : r + 1]
            nc.scalar.copy(
                out=repeated[:].rearrange("p (b i) -> p b i", i=QUADRANT),
                in_=picked.to_broadcast([P, words // QUADRANT, QUADRANT]),
            )
            wide = keep.tile([P, HIDDEN], BF16, name=name, align_bytes=64)
            nc.vector.transpose(out=wide[:].bitcast(F32), in_=repeated[:])
            return wide

        repeat_quadrant()
        nc.vector.transpose(out=turned_rows[:], in_=vec_quads[:].bitcast(F32))
        bias_i, gain_i, shift_i = spread(0, "bias_i"), spread(1, "gain_i"), spread(2, "shift_i")
        bias_c, gain_c, shift_c = spread(3, "bias_c"), spread(4, "gain_c"), spread(5, "shift_c")

        def mx_pass(acc, act_q, g, piece, first, w, cols, start, stop):
            codes, plane = act_q
            batch = slice(g * P, (g + 1) * P)
            nc.tensor.matmul_mx(
                out=acc[:],
                lhsT=codes[:, batch].bitcast(FP8X4),
                lhsT_scale=plane[:, batch],
                rhs=piece[:, cols.start - first : cols.stop - first].bitcast(FP8X4),
                rhs_scale=w_planes[4 * g : P, w, cols],
                start=start,
                stop=stop,
            )

        def add_bias(pre, acc, bias, cols):
            nc.vector.tensor_tensor(out=pre[:, cols], in0=acc[:], in1=bias[:, cols], op=ALU.add)

        def block_stats(stats, pre, j, cols):
            nc.vector.bn_stats(out=stats[:, j, :], in_=pre[:, cols])

        def mean_and_rstd(stats, name):
            mean_var = keep.tile([P, 2], F32, name=name + "_mean_var")
            nc.vector.bn_aggr(out=mean_var[:], in_=stats[:].rearrange("p j s -> p (j s)"))
            var_eps = keep.tile([P, 1], F32, name=name + "_var_eps")
            rstd = keep.tile([P, 1], F32, name=name + "_rstd")
            nc.gpsimd.tensor_scalar(
                out=var_eps[:], in0=mean_var[:, 1:2], scalar1=EPS, scalar2=None, op0=ALU.add
            )
            nc.gpsimd.tensor_tensor(out=rstd[:], in0=var_eps, in1=minus_half[:], op=ALU.pow)
            return mean_var[:, 0:1], rstd[:, 0:1]

        def centre_times_gain(pre, mean, gain, cols):
            nc.vector.scalar_tensor_tensor(
                out=pre[:, cols], in0=pre[:, cols], scalar=mean, in1=gain[:, cols],
                op0=ALU.subtract, op1=ALU.mult,
            )

        def scale_plus_shift(pre, rstd, shift, cols):
            nc.vector.scalar_tensor_tensor(
                out=pre[:, cols], in0=pre[:, cols], scalar=rstd, in1=shift[:, cols],
                op0=ALU.mult, op1=ALU.add,
            )

        acc_i = [psum_i.tile([P, BLOCK], F32, tag="bank", name="acc_i%d" % j) for j in range(BLOCKS)]
        for g in range(PASSES):
            for j in range(BLOCKS):
                mx_pass(acc_i[j], x_q, g, wi[g], 0, 0, block_cols(j), start=(g == 0), stop=False)
        for g in range(PASSES):
            for j in range(BLOCKS):
                mx_pass(
                    acc_i[j], h_q, g, ui[g], 0, 1, block_cols(j), start=False, stop=(g == PASSES - 1)
                )

        gate_i = keep.tile([P, HIDDEN], F32)
        stats_i = keep.tile([P, BLOCKS, 6], F32)
        for j in range(BLOCKS):
            add_bias(gate_i, acc_i[j], bias_i, block_cols(j))
        for j in range(BLOCKS):
            block_stats(stats_i, gate_i, j, block_cols(j))
        mean_i, rstd_i = mean_and_rstd(stats_i, "i")
        for j in range(BLOCKS):
            centre_times_gain(gate_i, mean_i, gain_i, block_cols(j))

        def finish_gate():
            for j in range(BLOCKS):
                scale_plus_shift(gate_i, rstd_i, shift_i, block_cols(j))
                nc.scalar.activation(
                    out=gate_i[:, block_cols(j)], in_=gate_i[:, block_cols(j)], func=ACT.Sigmoid
                )

        cand = keep.tile([P, HIDDEN], F32)
        scaled = keep.tile([P, TENSOR_BLOCKS * BLOCK], F32)
        stats_c = keep.tile([P, 6 * len(CAND_BLOCKS) + 3], F32)
        eps_record = stats_c[:, 6 * len(CAND_BLOCKS) :]
        nc.vector.memset(eps_record, 0.0)
        nc.vector.tensor_scalar(
            out=eps_record[:, 2:3], in0=eps_record[:, 2:3], scalar1=HIDDEN * EPS, scalar2=None, op0=ALU.add
        )
        mean_var = keep.tile([P, 2], F32)
        rstd = keep.tile([P, 1], F32)
        coef_rows = keep.tile([P, P], BF16)
        cand_cols = [slice(first, first + width) for first, width in CAND_BLOCKS]
        on_tensor, on_vector = cand_cols[:TENSOR_BLOCKS], cand_cols[TENSOR_BLOCKS:]

        acc_c = {}

        def x_passes(half, passes):
            first, pieces = wc[half]
            for g in passes:
                for b, cols in enumerate(cand_cols):
                    if first <= cols.start < first + HIDDEN // 2:
                        if g == 0:
                            pool = psum_i if b == len(cand_cols) - 1 else psum
                            acc = pool.tile([P, cols.stop - cols.start], F32, tag="bank", name="acc_c%d" % b)
                            acc_c[b] = acc
                        mx_pass(acc_c[b], x_q, g, pieces[g], first, 2, cols, start=(g == 0), stop=False)

        def h_passes(load):
            first, pieces = uc[load]
            for g in range(PASSES):
                for b, cols in enumerate(cand_cols):
                    if first <= cols.start < first + U_RANGES[load][1]:
                        mx_pass(
                            acc_c[b], h_q, g, pieces[g], first, 3, cols,
                            start=False, stop=(g == PASSES - 1),
                        )

        def add_block_bias(b):
            add_bias(cand, acc_c[b], bias_c, cand_cols[b])

        def take_stats(b):
            nc.vector.bn_stats(out=stats_c[:, 6 * b : 6 * b + 6], in_=cand[:, cand_cols[b]])

        arg = []

        def scale_block(engine, b):
            cols = cand_cols[b]
            engine.tensor_tensor(
                out=scaled[:, cols], in0=cand[:, cols], in1=gain_c[:, cols], op=ALU.mult
            )

        def open_arg(b):
            cols = cand_cols[b]
            bank = psum_i.tile([P, BLOCK], F32, tag="bank", name="arg%d" % b)
            nc.tensor.matmul(
                out=bank[:], lhsT=ident_f32[:], rhs=scaled[:, cols], start=True, stop=False
            )
            arg.append(bank)

        x_passes(0, range(PASSES))
        h_passes(0)
        add_block_bias(0)
        add_block_bias(1)
        for b in range(2):
            scale_block(nc.vector, b)
        for b in range(2):
            take_stats(b)
        finish_gate()
        x_passes(1, range(2))
        open_arg(0)
        open_arg(1)
        x_passes(1, range(2, PASSES))
        h_passes(1)
        add_block_bias(2)
        scale_block(nc.gpsimd, 2)
        h_passes(2)
        add_block_bias(3)
        take_stats(2)
        h_passes(3)
        add_block_bias(4)
        take_stats(3)
        take_stats(4)
        open_arg(2)

        nc.vector.bn_aggr(out=mean_var[:], in_=stats_c[:])
        mean, var_eps = mean_var[:, 0:1], mean_var[:, 1:2]
        nc.gpsimd.tensor_tensor(out=rstd[:], in0=var_eps, in1=minus_half[:], op=ALU.pow)
        gain_hi, gain_lo = coef[:, 4:5], coef[:, QUADRANT + 4 : QUADRANT + 5]
        shift_hi, shift_lo = coef[:, 5:6], coef[:, QUADRANT + 5 : QUADRANT + 6]
        nc.vector.tensor_scalar(out=gain_hi, in0=mean, scalar1=-1.0, scalar2=None, op0=ALU.mult)
        centre_times_gain(cand, mean, gain_c, on_vector[0])
        nc.vector.scalar_tensor_tensor(
            out=gain_lo, in0=mean, scalar=-1.0, in1=gain_hi, op0=ALU.mult, op1=ALU.subtract
        )
        centre_times_gain(cand, mean, gain_c, on_vector[1])
        nc.vector.tensor_tensor(out=shift_hi, in0=var_eps, in1=rstd[:], op=ALU.mult)
        scale_plus_shift(cand, rstd[:], shift_c, on_vector[0])
        nc.vector.scalar_tensor_tensor(
            out=shift_lo, in0=var_eps, scalar=rstd[:], in1=shift_hi, op0=ALU.mult, op1=ALU.subtract
        )
        scale_plus_shift(cand, rstd[:], shift_c, on_vector[1])
        turned = psum.tile([P, P], BF16, tag="bank", name="turned")
        nc.tensor.transpose(turned[:], coef[:], ident_bf16[:])
        for i, cols in enumerate(on_vector):
            nc.scalar.activation(out=cand[:, cols], in_=cand[:, cols], func=ACT.Tanh)
            if i == 0:
                nc.scalar.copy(out=coef_rows[:], in_=turned[:])
        for bank, cols in zip(arg, on_tensor):
            nc.tensor.matmul(
                out=bank[:], lhsT=coef_rows[:], rhs=vec_quads[:, cols], start=False, stop=True
            )
        cut = BLOCK // 2
        parts = [(arg[0], 0, BLOCK), (arg[1], 0, BLOCK), (arg[2], 0, cut), (arg[2], cut, BLOCK)]
        finished = list(on_vector)
        for b, (bank, start, stop) in zip((0, 1, 2, 2), parts):
            cols = slice(b * BLOCK + start, b * BLOCK + stop)
            nc.scalar.activation(
                out=cand[:, cols], in_=bank[:, start:stop], func=ACT.Tanh, scale=rstd[:]
            )
            finished.append(cols)
        for cols in finished:
            nc.vector.tensor_tensor(
                out=cand[:, cols], in0=cand[:, cols], in1=gate_i[:, cols], op=ALU.mult
            )
            nc.sync.dma_start(out=out[:, cols], in_=cand[:, cols])
